import numpy as np
import ml_dtypes


def mxq(x, axis, fmt="e4m3"):
    dtype, down = {"e4m3": (ml_dtypes.float8_e4m3fn, 7), "e5m2": (ml_dtypes.float8_e5m2, 14)}[fmt]
    v = np.moveaxis(np.asarray(x, np.float32).astype(ml_dtypes.bfloat16).astype(np.float64), axis, -1)
    blocks = v.reshape(v.shape[:-1] + (-1, 32))
    amax = np.abs(blocks).max(-1, keepdims=True)
    byte = np.maximum(np.where(amax > 0, np.frexp(amax)[1] - 1 + 127, 0) - down, 1)
    scale = np.exp2(byte - 127.0)
    codes = (blocks / scale).astype(np.float32).astype(dtype).astype(np.float64)
    return np.moveaxis((codes * scale).reshape(v.shape), -1, axis)


WIDE = False


def mx_kscale(k):
    if not WIDE:
        return np.ones(k)
    levels = np.array([10, -10, 5, -5, 0])
    if k % 512:
        return np.exp2(np.random.permutation(np.resize(levels, k // 32))).repeat(32)
    a = np.empty((k // 512, 16))
    for p in range(k // 512):
        a[p, :8] = np.random.permutation(np.resize(levels, 8))
        for g in range(8):
            far = levels[np.abs(levels - a[p, g]) >= 10]
            a[p, g + 8] = far[np.random.randint(len(far))]
    return np.exp2(a.ravel()).repeat(32)


BF16 = ml_dtypes.bfloat16


def bf(x):
    return np.asarray(x, np.float32).astype(BF16)


def f64(x):
    return np.asarray(x).astype(np.float64)


B, K, D, H1, H2, C = 2048, 2, 1024, 256, 512, 64
N = B * K


def setup_inputs():
    s = mx_kscale(D)
    return {"nf1": bf(np.random.standard_normal((N, D)) * s),
            "nf2": bf(np.random.standard_normal((N * K, D)) * s),
            "w1_0": bf(np.random.standard_normal((D, H1)) / np.sqrt(D) / s[:, None]),
            "w2_0": bf(np.random.standard_normal((D, H1)) / np.sqrt(D) / s[:, None])}


def sage_gcn(cur, neigh, w1, w2):
    b, d = cur.shape
    agg = neigh.reshape(b, -1, d).mean(axis=1)
    return np.maximum((mxq(cur, 1, "e4m3") @ mxq(w2, 0, "e4m3")) + (mxq(agg, 1, "e4m3") @ mxq(w1, 0, "e4m3")), 0.0)


def reference(nf1, nf2, w1_0, w2_0):
    return sage_gcn(f64(nf1), f64(nf2), f64(w1_0), f64(w2_0))

@@ -1,0 +1,169 @@
+from contextlib import ExitStack
+
+import concourse.mybir as mybir
+from concourse.masks import make_identity
+
+F32 = mybir.dt.float32
+BF16 = mybir.dt.bfloat16
+U32 = mybir.dt.uint32
+U8 = mybir.dt.uint8
+FP8X4 = mybir.dt.float8_e4m3fn_x4
+ACT = mybir.ActivationFunctionType
+ALU = mybir.AluOpType
+
+P = 128
+PACK = 4
+K_PASS = P * PACK
+HALVES = 2
+PAIR = 2
+
+NODES = 4096
+NEIGHBOURS = 2
+D = 1024
+H = 256
+PASSES = D // K_PASS
+WORDS = D // PAIR
+
+TILES = 2
+GROUPS = NODES // (P * TILES)
+LOAD_AHEAD = 6
+
+FLOPS = 2 * 2 * NODES * D * H
+
+
+def quantise_weight(nc, const, w, copy, name):
+    raw = const.tile([P, PASSES * PACK * H], BF16, name=name + "_raw")
+    nc.scalar.dma_start(
+        out=raw[:].rearrange("p (g t c) -> p g t c", t=PACK, c=H),
+        in_=w.rearrange("(g p t) c -> p g t c", p=P, t=PACK),
+    )
+    grouped = const.tile([P, PASSES * H * PACK], BF16, name=name + "_grouped", align_bytes=64)
+    copy(
+        out=grouped[:].rearrange("p (g c t) -> p g c t", g=PASSES, t=PACK),
+        in_=raw[:].rearrange("p (g t c) -> p g c t", g=PASSES, t=PACK),
+    )
+    codes = const.tile([P, PASSES * H], U32, name=name + "_codes", align_bytes=64)
+    scales = const.tile([P, PASSES * H], U8, name=name + "_scales", align_bytes=64)
+    nc.vector.quantize_mx(out=codes[:].bitcast(FP8X4), scales=scales[:], in_=grouped[:])
+    return codes, scales
+
+
+def tile_graphsage_pa_t_kernel(tc, nf1, nf2, w1_0, w2_0, out):
+    nc = tc.nc
+
+    own_rows = nf1.rearrange("(p j) d -> p (j d)", p=P)
+    neighbour_rows = nf2.rearrange("(p j) d -> p (j d)", p=P)
+    out_rows = out.rearrange("(p j) h -> p (j h)", p=P)
+
+    with ExitStack() as ctx:
+        ctx.enter_context(tc.manual_schedule())
+        const = ctx.enter_context(tc.tile_pool(name="const", bufs=1))
+        loads = ctx.enter_context(tc.tile_pool(name="loads", bufs=LOAD_AHEAD))
+        work = ctx.enter_context(tc.tile_pool(name="work", bufs=3))
+        psum_t = ctx.enter_context(tc.psum_pool(name="psum_t", bufs=3))
+        psum_acc = ctx.enter_context(tc.psum_pool(name="psum_acc", bufs=2))
+
+        def columns_of(rows, first_group, end_group):
+            width = rows.shape[1] // GROUPS
+            return rows[:, first_group * width : end_group * width]
+
+        def load(g):
+            neighbours = loads.tile([P, TILES * NEIGHBOURS * D], BF16, name="neighbours")
+            nc.sync.dma_start(out=neighbours[:], in_=columns_of(neighbour_rows, g, g + 1))
+            own = loads.tile([P, TILES * D], BF16, name="own")
+            nc.sync.dma_start(out=own[:], in_=columns_of(own_rows, g, g + 1))
+            return neighbours, own
+
+        def mean_of_neighbours(neighbours):
+            both = neighbours[:].rearrange("p (r j d) -> p r j d", r=TILES, j=NEIGHBOURS)
+            pair_sum = work.tile([P, TILES * D], BF16, name="pair_sum")
+            nc.vector.tensor_tensor(
+                out=pair_sum[:].rearrange("p (r d) -> p r d", r=TILES),
+                in0=both[:, :, 0, :],
+                in1=both[:, :, 1, :],
+                op=ALU.add,
+            )
+            mean = work.tile([P, TILES * D], BF16, name="mean")
+            nc.vector.tensor_scalar_mul(out=mean[:], in0=pair_sum[:], scalar1=1.0 / NEIGHBOURS)
+            return mean
+
+        def transpose_words(rows, r, name):
+            words = rows[:].bitcast(F32)
+            bank = psum_t.tile([P, WORDS], F32, name=name)
+            for g in range(PASSES):
+                for u in range(HALVES):
+                    first = r * WORDS + g * HALVES * P
+                    nc.tensor.transpose(
+                        bank[:, (u * PASSES + g) * P : (u * PASSES + g + 1) * P],
+                        words[:, first + u : first + HALVES * P : HALVES],
+                        identity[:],
+                    )
+            return bank
+
+        def transpose_group(rows, name):
+            banks = [transpose_words(rows, r, name + "_t") for r in range(TILES)]
+            grouped = work.tile([P, TILES * D], BF16, name=name + "_grouped", align_bytes=64)
+            for r in range(TILES):
+                nc.scalar.copy(
+                    out=grouped[:]
+                    .bitcast(F32)[:, r * WORDS : (r + 1) * WORDS]
+                    .rearrange("p (n u) -> p n u", u=HALVES),
+                    in_=banks[r][:].rearrange("p (u n) -> p n u", u=HALVES),
+                )
+            return grouped
+
+        def quantise(grouped, name):
+            codes = work.tile([P, TILES * D // PACK], U32, name=name + "_codes", align_bytes=64)
+            scales = work.tile([P, TILES * D // PACK], U8, name=name + "_scales", align_bytes=64)
+            nc.vector.quantize_mx(out=codes[:].bitcast(FP8X4), scales=scales[:], in_=grouped[:])
+            return codes, scales
+
+        def multiply(group, own_q, mean_q):
+            products = ((own_q, w2_q), (mean_q, w1_q))
+            acc = psum_acc.tile([P, TILES * H], F32, name="acc")
+            for r in range(TILES):
+                for i, (x_q, w_q) in enumerate(products):
+                    for g in range(PASSES):
+                        nodes = slice((r * PASSES + g) * P, (r * PASSES + g + 1) * P)
+                        cols = slice(g * H, (g + 1) * H)
+                        nc.tensor.matmul_mx(
+                            out=acc[:, r * H : (r + 1) * H],
+                            lhsT=x_q[0][:, nodes].bitcast(FP8X4),
+                            lhsT_scale=x_q[1][:, nodes],
+                            rhs=w_q[0][:, cols].bitcast(FP8X4),
+                            rhs_scale=w_q[1][:, cols],
+                            start=(i == 0 and g == 0),
+                            stop=(i == len(products) - 1 and g == PASSES - 1),
+                        )
+            nc.scalar.activation(
+                out=columns_of(results, group, group + 1), in_=acc[:], func=ACT.Relu
+            )
+
+        identity = const.tile([P, P], F32, name="identity")
+        make_identity(nc, identity[:])
+        results = const.tile([P, GROUPS * TILES * H], F32, name="results")
+        loaded = [load(g) for g in range(LOAD_AHEAD)]
+        means = [mean_of_neighbours(loaded[0][0])]
+        w2_q = quantise_weight(nc, const, w2_0, nc.vector.tensor_copy, "w2")
+        w1_q = quantise_weight(nc, const, w1_0, nc.scalar.copy, "w1")
+
+        quantised = []
+        stored = 0
+        for g in range(GROUPS + 1):
+            if g + 1 < GROUPS:
+                means.append(mean_of_neighbours(loaded[g + 1][0]))
+            if g < GROUPS:
+                own_grouped = transpose_group(loaded[g][1], "own")
+                mean_grouped = transpose_group(means[g], "mean")
+                own_q = quantise(own_grouped, "own")
+                mean_q = quantise(mean_grouped, "mean")
+                quantised.append((own_q, mean_q))
+            if g > 0:
+                multiply(g - 1, quantised[g - 1][0], quantised[g - 1][1])
+            if g + LOAD_AHEAD < GROUPS:
+                loaded.append(load(g + LOAD_AHEAD))
+            else:
+                nc.sync.dma_start(
+                    out=columns_of(out_rows, stored, g), in_=columns_of(results, stored, g)
+                )
+                stored = g

@@ -74,7 +74,7 @@ def tile_graphsage_pa_t_kernel(tc, nf1, nf2, w1_0, w2_0, out):
             nc.sync.dma_start(out=own[:], in_=columns_of(own_rows, g, g + 1))
             return neighbours, own
 
-        def mean_of_neighbours(neighbours):
+        def sum_of_neighbours(neighbours):
             both = neighbours[:].rearrange("p (r j d) -> p r j d", r=TILES, j=NEIGHBOURS)
             pair_sum = work.tile([P, TILES * D], BF16, name="pair_sum")
             nc.vector.tensor_tensor(
@@ -83,9 +83,10 @@ def tile_graphsage_pa_t_kernel(tc, nf1, nf2, w1_0, w2_0, out):
                 in1=both[:, :, 1, :],
                 op=ALU.add,
             )
-            mean = work.tile([P, TILES * D], BF16, name="mean")
-            nc.vector.tensor_scalar_mul(out=mean[:], in0=pair_sum[:], scalar1=1.0 / NEIGHBOURS)
-            return mean
+            return pair_sum
+
+        def copy_of_half(out, in_):
+            nc.vector.tensor_scalar_mul(out=out, in0=in_, scalar1=1.0 / NEIGHBOURS)
 
         def transpose_words(rows, r, name):
             words = rows[:].bitcast(F32)
@@ -118,8 +119,8 @@ def tile_graphsage_pa_t_kernel(tc, nf1, nf2, w1_0, w2_0, out):
             nc.vector.quantize_mx(out=codes[:].bitcast(FP8X4), scales=scales[:], in_=grouped[:])
             return codes, scales
 
-        def multiply(group, own_q, mean_q):
-            products = ((own_q, w2_q), (mean_q, w1_q))
+        def multiply(group, own_q, sum_q):
+            products = ((own_q, w2_q), (sum_q, w1_q))
             acc = psum_acc.tile([P, TILES * H], F32, name="acc")
             for r in range(TILES):
                 for i, (x_q, w_q) in enumerate(products):
@@ -143,21 +144,21 @@ def tile_graphsage_pa_t_kernel(tc, nf1, nf2, w1_0, w2_0, out):
         make_identity(nc, identity[:])
         results = const.tile([P, GROUPS * TILES * H], F32, name="results")
         loaded = [load(g) for g in range(LOAD_AHEAD)]
-        means = [mean_of_neighbours(loaded[0][0])]
-        w2_q = quantise_weight(nc, const, w2_0, nc.vector.tensor_copy, "w2")
-        w1_q = quantise_weight(nc, const, w1_0, nc.scalar.copy, "w1")
+        sums = [sum_of_neighbours(loaded[0][0])]
+        w1_q = quantise_weight(nc, const, w1_0, copy_of_half, "w1")
+        w2_q = quantise_weight(nc, const, w2_0, nc.scalar.copy, "w2")
 
         quantised = []
         stored = 0
         for g in range(GROUPS + 1):
             if g + 1 < GROUPS:
-                means.append(mean_of_neighbours(loaded[g + 1][0]))
+                sums.append(sum_of_neighbours(loaded[g + 1][0]))
             if g < GROUPS:
                 own_grouped = transpose_group(loaded[g][1], "own")
-                mean_grouped = transpose_group(means[g], "mean")
+                sum_grouped = transpose_group(sums[g], "sum")
                 own_q = quantise(own_grouped, "own")
-                mean_q = quantise(mean_grouped, "mean")
-                quantised.append((own_q, mean_q))
+                sum_q = quantise(sum_grouped, "sum")
+                quantised.append((own_q, sum_q))
             if g > 0:
                 multiply(g - 1, quantised[g - 1][0], quantised[g - 1][1])
             if g + LOAD_AHEAD < GROUPS:

@@ -24,9 +24,25 @@ H = 256
 PASSES = D // K_PASS
 WORDS = D // PAIR
 
-TILES = 2
-GROUPS = NODES // (P * TILES)
-LOAD_AHEAD = 6
+TILES = NODES // P
+GROUP = 2
+GROUPS = [(t, GROUP) for t in range(0, TILES - GROUP, GROUP)] + [
+    (t, 1) for t in range(TILES - GROUP, TILES)
+]
+
+OWN, NEIGHBOUR = "own", "neighbours"
+OWN_LOAD = 8
+NEIGHBOUR_LOAD = 4
+LOADS = [
+    (OWN, 0, 2), (NEIGHBOUR, 0, 2), (NEIGHBOUR, 2, 2), (OWN, 2, 6), (NEIGHBOUR, 4, 4),
+    (OWN, 8, 8), (NEIGHBOUR, 8, 4), (NEIGHBOUR, 12, 4),
+    (OWN, 16, 8), (NEIGHBOUR, 16, 4), (NEIGHBOUR, 20, 4),
+    (OWN, 24, 8), (NEIGHBOUR, 24, 4), (NEIGHBOUR, 28, 2), (NEIGHBOUR, 30, 1), (NEIGHBOUR, 31, 1),
+]
+OWN_BUFS = 3
+NEIGHBOUR_BUFS = 5
+
+STORE_ENDS = (24, 30, 32)
 
 FLOPS = 2 * 2 * NODES * D * H
 
@@ -58,42 +74,53 @@ def tile_graphsage_pa_t_kernel(tc, nf1, nf2, w1_0, w2_0, out):
     with ExitStack() as ctx:
         ctx.enter_context(tc.manual_schedule())
         const = ctx.enter_context(tc.tile_pool(name="const", bufs=1))
-        loads = ctx.enter_context(tc.tile_pool(name="loads", bufs=LOAD_AHEAD))
+        own_pool = ctx.enter_context(tc.tile_pool(name="own_pool", bufs=OWN_BUFS))
+        neighbour_pool = ctx.enter_context(
+            tc.tile_pool(name="neighbour_pool", bufs=NEIGHBOUR_BUFS)
+        )
         work = ctx.enter_context(tc.tile_pool(name="work", bufs=3))
         psum_t = ctx.enter_context(tc.psum_pool(name="psum_t", bufs=3))
         psum_acc = ctx.enter_context(tc.psum_pool(name="psum_acc", bufs=2))
 
-        def columns_of(rows, first_group, end_group):
-            width = rows.shape[1] // GROUPS
-            return rows[:, first_group * width : end_group * width]
+        loaded = {OWN: {}, NEIGHBOUR: {}}
 
-        def load(g):
-            neighbours = loads.tile([P, TILES * NEIGHBOURS * D], BF16, name="neighbours")
-            nc.sync.dma_start(out=neighbours[:], in_=columns_of(neighbour_rows, g, g + 1))
-            own = loads.tile([P, TILES * D], BF16, name="own")
-            nc.sync.dma_start(out=own[:], in_=columns_of(own_rows, g, g + 1))
-            return neighbours, own
+        def load(kind, first, count):
+            if kind == OWN:
+                width, rows, pool, longest = D, own_rows, own_pool, OWN_LOAD
+            else:
+                width, rows, pool, longest = NEIGHBOURS * D, neighbour_rows, neighbour_pool, NEIGHBOUR_LOAD
+            landing = pool.tile([P, longest * width], BF16, name=kind)
+            nc.sync.dma_start(
+                out=landing[:, : count * width],
+                in_=rows[:, first * width : (first + count) * width],
+            )
+            for j in range(count):
+                loaded[kind][first + j] = (landing, j * width)
 
-        def sum_of_neighbours(neighbours):
-            both = neighbours[:].rearrange("p (r j d) -> p r j d", r=TILES, j=NEIGHBOURS)
-            pair_sum = work.tile([P, TILES * D], BF16, name="pair_sum")
+        def sum_of_neighbours(group):
+            first, count = group
+            landing, column = loaded[NEIGHBOUR][first]
+            both = landing[:, column : column + count * NEIGHBOURS * D].rearrange(
+                "p (r j d) -> p r j d", r=count, j=NEIGHBOURS
+            )
+            pair_sum = work.tile([P, GROUP * D], BF16, name="pair_sum")
             nc.vector.tensor_tensor(
-                out=pair_sum[:].rearrange("p (r d) -> p r d", r=TILES),
+                out=pair_sum[:, : count * D].rearrange("p (r d) -> p r d", r=count),
                 in0=both[:, :, 0, :],
                 in1=both[:, :, 1, :],
                 op=ALU.add,
             )
-            return pair_sum
+            return pair_sum, 0
 
         def copy_of_half(out, in_):
             nc.vector.tensor_scalar_mul(out=out, in0=in_, scalar1=1.0 / NEIGHBOURS)
 
-        def transpose_words(rows, r, name):
+        def transpose_words(rows, column, name):
             words = rows[:].bitcast(F32)
             bank = psum_t.tile([P, WORDS], F32, name=name)
             for g in range(PASSES):
                 for u in range(HALVES):
-                    first = r * WORDS + g * HALVES * P
+                    first = column // PAIR + g * HALVES * P
                     nc.tensor.transpose(
                         bank[:, (u * PASSES + g) * P : (u * PASSES + g + 1) * P],
                         words[:, first + u : first + HALVES * P : HALVES],
@@ -101,10 +128,11 @@ def tile_graphsage_pa_t_kernel(tc, nf1, nf2, w1_0, w2_0, out):
                     )
             return bank
 
-        def transpose_group(rows, name):
-            banks = [transpose_words(rows, r, name + "_t") for r in range(TILES)]
-            grouped = work.tile([P, TILES * D], BF16, name=name + "_grouped", align_bytes=64)
-            for r in range(TILES):
+        def transpose_group(source, count, name):
+            rows, column = source
+            banks = [transpose_words(rows, column + r * D, name + "_t") for r in range(count)]
+            grouped = work.tile([P, GROUP * D], BF16, name=name + "_grouped", align_bytes=64)
+            for r in range(count):
                 nc.scalar.copy(
                     out=grouped[:]
                     .bitcast(F32)[:, r * WORDS : (r + 1) * WORDS]
@@ -113,16 +141,22 @@ def tile_graphsage_pa_t_kernel(tc, nf1, nf2, w1_0, w2_0, out):
                 )
             return grouped
 
-        def quantise(grouped, name):
-            codes = work.tile([P, TILES * D // PACK], U32, name=name + "_codes", align_bytes=64)
-            scales = work.tile([P, TILES * D // PACK], U8, name=name + "_scales", align_bytes=64)
-            nc.vector.quantize_mx(out=codes[:].bitcast(FP8X4), scales=scales[:], in_=grouped[:])
+        def quantise(grouped, count, name):
+            codes = work.tile([P, GROUP * D // PACK], U32, name=name + "_codes", align_bytes=64)
+            scales = work.tile([P, GROUP * D // PACK], U8, name=name + "_scales", align_bytes=64)
+            width = count * D // PACK
+            nc.vector.quantize_mx(
+                out=codes[:, :width].bitcast(FP8X4),
+                scales=scales[:, :width],
+                in_=grouped[:, : count * D],
+            )
             return codes, scales
 
         def multiply(group, own_q, sum_q):
+            first, count = group
             products = ((own_q, w2_q), (sum_q, w1_q))
-            acc = psum_acc.tile([P, TILES * H], F32, name="acc")
-            for r in range(TILES):
+            acc = psum_acc.tile([P, GROUP * H], F32, name="acc")
+            for r in range(count):
                 for i, (x_q, w_q) in enumerate(products):
                     for g in range(PASSES):
                         nodes = slice((r * PASSES + g) * P, (r * PASSES + g + 1) * P)
@@ -137,34 +171,59 @@ def tile_graphsage_pa_t_kernel(tc, nf1, nf2, w1_0, w2_0, out):
                             stop=(i == len(products) - 1 and g == PASSES - 1),
                         )
             nc.scalar.activation(
-                out=columns_of(results, group, group + 1), in_=acc[:], func=ACT.Relu
+                out=results[:, first * H : (first + count) * H],
+                in_=acc[:, : count * H],
+                func=ACT.Relu,
             )
 
         identity = const.tile([P, P], F32, name="identity")
         make_identity(nc, identity[:])
-        results = const.tile([P, GROUPS * TILES * H], F32, name="results")
-        loaded = [load(g) for g in range(LOAD_AHEAD)]
-        sums = [sum_of_neighbours(loaded[0][0])]
+        results = const.tile([P, TILES * H], F32, name="results")
+
+        pending = list(LOADS)
+        bufs = {OWN: OWN_BUFS, NEIGHBOUR: NEIGHBOUR_BUFS}
+        issued = {OWN: [], NEIGHBOUR: []}
+
+        def issue_loads(read):
+            while pending:
+                kind, first, count = pending[0]
+                if len(issued[kind]) >= bufs[kind] and issued[kind][-bufs[kind]] > read[kind]:
+                    return
+                pending.remove(pending[0])
+                load(kind, first, count)
+                issued[kind].append(first + count)
+
+        issue_loads({OWN: 0, NEIGHBOUR: 0})
+        sums = [sum_of_neighbours(GROUPS[0])]
         w1_q = quantise_weight(nc, const, w1_0, copy_of_half, "w1")
         w2_q = quantise_weight(nc, const, w2_0, nc.scalar.copy, "w2")
 
-        quantised = []
+        def own_codes(group):
+            grouped = transpose_group(loaded[OWN][group[0]], group[1], "own")
+            return lambda: quantise(grouped, group[1], "own")
+
+        own_q = [own_codes(GROUPS[0])()]
+        sum_q = []
         stored = 0
-        for g in range(GROUPS + 1):
-            if g + 1 < GROUPS:
-                sums.append(sum_of_neighbours(loaded[g + 1][0]))
-            if g < GROUPS:
-                own_grouped = transpose_group(loaded[g][1], "own")
-                sum_grouped = transpose_group(sums[g], "sum")
-                own_q = quantise(own_grouped, "own")
-                sum_q = quantise(sum_grouped, "sum")
-                quantised.append((own_q, sum_q))
+        for g in range(len(GROUPS) + 1):
+            quantise_later = []
+            if g + 1 < len(GROUPS):
+                sums.append(sum_of_neighbours(GROUPS[g + 1]))
+            if g < len(GROUPS):
+                first, count = GROUPS[g]
+                sum_grouped = transpose_group(sums[g], count, "sum")
+                if g + 1 < len(GROUPS):
+                    quantise_later.append(own_codes(GROUPS[g + 1]))
+                sum_q.append(quantise(sum_grouped, count, "sum"))
+                own_q.extend([step() for step in quantise_later])
             if g > 0:
-                multiply(g - 1, quantised[g - 1][0], quantised[g - 1][1])
-            if g + LOAD_AHEAD < GROUPS:
-                loaded.append(load(g + LOAD_AHEAD))
-            else:
+                multiply(GROUPS[g - 1], own_q[g - 1], sum_q[g - 1])
+            if g + 1 < len(GROUPS):
+                read = sum(GROUPS[g + 1])
+                issue_loads({OWN: read, NEIGHBOUR: read})
+            done = sum(GROUPS[g - 1]) if g > 0 else 0
+            if done in STORE_ENDS:
                 nc.sync.dma_start(
-                    out=columns_of(out_rows, stored, g), in_=columns_of(results, stored, g)
+                    out=out_rows[:, stored * H : done * H], in_=results[:, stored * H : done * H]
                 )
-                stored = g
+                stored = done

@@ -15,6 +15,7 @@ P = 128
 PACK = 4
 K_PASS = P * PACK
 HALVES = 2
+BLOCK = 32
 PAIR = 2
 
 NODES = 4096
@@ -31,28 +32,37 @@ GROUPS = [(t, GROUP) for t in range(0, TILES - GROUP, GROUP)] + [
 ]
 
 OWN, NEIGHBOUR = "own", "neighbours"
-OWN_LOAD = 8
-NEIGHBOUR_LOAD = 4
+LOAD = 2
 LOADS = [
-    (OWN, 0, 2), (NEIGHBOUR, 0, 2), (NEIGHBOUR, 2, 2), (OWN, 2, 6), (NEIGHBOUR, 4, 4),
-    (OWN, 8, 8), (NEIGHBOUR, 8, 4), (NEIGHBOUR, 12, 4),
-    (OWN, 16, 8), (NEIGHBOUR, 16, 4), (NEIGHBOUR, 20, 4),
-    (OWN, 24, 8), (NEIGHBOUR, 24, 4), (NEIGHBOUR, 28, 2), (NEIGHBOUR, 30, 1), (NEIGHBOUR, 31, 1),
-]
-OWN_BUFS = 3
-NEIGHBOUR_BUFS = 5
+    (kind, t, LOAD) for t in range(0, TILES - LOAD, LOAD) for kind in (OWN, NEIGHBOUR)
+] + [(OWN, TILES - LOAD, LOAD)] + [(NEIGHBOUR, t, 1) for t in range(TILES - LOAD, TILES)]
+LOAD_BUFS = 8
 
 STORE_ENDS = (24, 30, 32)
 
 FLOPS = 2 * 2 * NODES * D * H
 
 
-def quantise_weight(nc, const, w, copy, name):
-    raw = const.tile([P, PASSES * PACK * H], BF16, name=name + "_raw")
+def load_in_word_order(nc, raw, w):
     nc.scalar.dma_start(
         out=raw[:].rearrange("p (g t c) -> p g t c", t=PACK, c=H),
         in_=w.rearrange("(g p t) c -> p g t c", p=P, t=PACK),
     )
+
+
+def load_in_run_order(nc, raw, w):
+    halves = raw[:].rearrange("p (s x) -> p s x", s=PASSES * HALVES)
+    rows = w.rearrange(
+        "(g q u i e) c -> g u q i (e c)", g=PASSES, u=HALVES, i=BLOCK // HALVES // PAIR, e=PAIR
+    )
+    for g in range(PASSES):
+        for u in range(HALVES):
+            nc.scalar.dma_start(out=halves[:, g * HALVES + u, :], in_=rows[g, u])
+
+
+def quantise_weight(nc, const, w, load, copy, name):
+    raw = const.tile([P, PASSES * PACK * H], BF16, name=name + "_raw")
+    load(nc, raw, w)
     grouped = const.tile([P, PASSES * H * PACK], BF16, name=name + "_grouped", align_bytes=64)
     copy(
         out=grouped[:].rearrange("p (g c t) -> p g c t", g=PASSES, t=PACK),
@@ -74,10 +84,8 @@ def tile_graphsage_pa_t_kernel(tc, nf1, nf2, w1_0, w2_0, out):
     with ExitStack() as ctx:
         ctx.enter_context(tc.manual_schedule())
         const = ctx.enter_context(tc.tile_pool(name="const", bufs=1))
-        own_pool = ctx.enter_context(tc.tile_pool(name="own_pool", bufs=OWN_BUFS))
-        neighbour_pool = ctx.enter_context(
-            tc.tile_pool(name="neighbour_pool", bufs=NEIGHBOUR_BUFS)
-        )
+        own_pool = ctx.enter_context(tc.tile_pool(name="own_pool", bufs=LOAD_BUFS))
+        neighbour_pool = ctx.enter_context(tc.tile_pool(name="neighbour_pool", bufs=LOAD_BUFS))
         work = ctx.enter_context(tc.tile_pool(name="work", bufs=3))
         psum_t = ctx.enter_context(tc.psum_pool(name="psum_t", bufs=3))
         psum_acc = ctx.enter_context(tc.psum_pool(name="psum_acc", bufs=2))
@@ -86,10 +94,10 @@ def tile_graphsage_pa_t_kernel(tc, nf1, nf2, w1_0, w2_0, out):
 
         def load(kind, first, count):
             if kind == OWN:
-                width, rows, pool, longest = D, own_rows, own_pool, OWN_LOAD
+                width, rows, pool = D, own_rows, own_pool
             else:
-                width, rows, pool, longest = NEIGHBOURS * D, neighbour_rows, neighbour_pool, NEIGHBOUR_LOAD
-            landing = pool.tile([P, longest * width], BF16, name=kind)
+                width, rows, pool = NEIGHBOURS * D, neighbour_rows, neighbour_pool
+            landing = pool.tile([P, LOAD * width], BF16, name=kind)
             nc.sync.dma_start(
                 out=landing[:, : count * width],
                 in_=rows[:, first * width : (first + count) * width],
@@ -99,38 +107,46 @@ def tile_graphsage_pa_t_kernel(tc, nf1, nf2, w1_0, w2_0, out):
 
         def sum_of_neighbours(group):
             first, count = group
-            landing, column = loaded[NEIGHBOUR][first]
-            both = landing[:, column : column + count * NEIGHBOURS * D].rearrange(
-                "p (r j d) -> p r j d", r=count, j=NEIGHBOURS
-            )
             pair_sum = work.tile([P, GROUP * D], BF16, name="pair_sum")
-            nc.vector.tensor_tensor(
-                out=pair_sum[:, : count * D].rearrange("p (r d) -> p r d", r=count),
-                in0=both[:, :, 0, :],
-                in1=both[:, :, 1, :],
-                op=ALU.add,
-            )
+            for r in range(count):
+                landing, column = loaded[NEIGHBOUR][first + r]
+                both = landing[:, column : column + NEIGHBOURS * D].rearrange(
+                    "p (j b u x) -> p j u b x", j=NEIGHBOURS, u=HALVES, b=D // BLOCK
+                )
+                nc.vector.tensor_tensor(
+                    out=pair_sum[:, r * D : (r + 1) * D].rearrange(
+                        "p (u b x) -> p u b x", u=HALVES, b=D // BLOCK
+                    ),
+                    in0=both[:, 0],
+                    in1=both[:, 1],
+                    op=ALU.add,
+                )
             return pair_sum, 0
 
         def copy_of_half(out, in_):
             nc.vector.tensor_scalar_mul(out=out, in0=in_, scalar1=1.0 / NEIGHBOURS)
 
-        def transpose_words(rows, column, name):
-            words = rows[:].bitcast(F32)
+        def own_words(g, u):
+            return slice(g * HALVES * P + u, (g + 1) * HALVES * P, HALVES)
+
+        def sum_words(g, u):
+            return slice((u * PASSES + g) * P, (u * PASSES + g + 1) * P)
+
+        def transpose_words(rows, column, where, name):
+            words = rows[:].bitcast(F32)[:, column // PAIR : column // PAIR + WORDS]
             bank = psum_t.tile([P, WORDS], F32, name=name)
             for g in range(PASSES):
                 for u in range(HALVES):
-                    first = column // PAIR + g * HALVES * P
                     nc.tensor.transpose(
                         bank[:, (u * PASSES + g) * P : (u * PASSES + g + 1) * P],
-                        words[:, first + u : first + HALVES * P : HALVES],
+                        words[:, where(g, u)],
                         identity[:],
                     )
             return bank
 
-        def transpose_group(source, count, name):
+        def transpose_group(source, count, where, name):
             rows, column = source
-            banks = [transpose_words(rows, column + r * D, name + "_t") for r in range(count)]
+            banks = [transpose_words(rows, column + r * D, where, name + "_t") for r in range(count)]
             grouped = work.tile([P, GROUP * D], BF16, name=name + "_grouped", align_bytes=64)
             for r in range(count):
                 nc.scalar.copy(
@@ -181,25 +197,24 @@ def tile_graphsage_pa_t_kernel(tc, nf1, nf2, w1_0, w2_0, out):
         results = const.tile([P, TILES * H], F32, name="results")
 
         pending = list(LOADS)
-        bufs = {OWN: OWN_BUFS, NEIGHBOUR: NEIGHBOUR_BUFS}
         issued = {OWN: [], NEIGHBOUR: []}
 
         def issue_loads(read):
             while pending:
                 kind, first, count = pending[0]
-                if len(issued[kind]) >= bufs[kind] and issued[kind][-bufs[kind]] > read[kind]:
+                if len(issued[kind]) >= LOAD_BUFS and issued[kind][-LOAD_BUFS] > read:
                     return
                 pending.remove(pending[0])
                 load(kind, first, count)
                 issued[kind].append(first + count)
 
-        issue_loads({OWN: 0, NEIGHBOUR: 0})
+        issue_loads(0)
         sums = [sum_of_neighbours(GROUPS[0])]
-        w1_q = quantise_weight(nc, const, w1_0, copy_of_half, "w1")
-        w2_q = quantise_weight(nc, const, w2_0, nc.scalar.copy, "w2")
+        w1_q = quantise_weight(nc, const, w1_0, load_in_run_order, copy_of_half, "w1")
+        w2_q = quantise_weight(nc, const, w2_0, load_in_word_order, nc.scalar.copy, "w2")
 
         def own_codes(group):
-            grouped = transpose_group(loaded[OWN][group[0]], group[1], "own")
+            grouped = transpose_group(loaded[OWN][group[0]], group[1], own_words, "own")
             return lambda: quantise(grouped, group[1], "own")
 
         own_q = [own_codes(GROUPS[0])()]
@@ -211,7 +226,7 @@ def tile_graphsage_pa_t_kernel(tc, nf1, nf2, w1_0, w2_0, out):
                 sums.append(sum_of_neighbours(GROUPS[g + 1]))
             if g < len(GROUPS):
                 first, count = GROUPS[g]
-                sum_grouped = transpose_group(sums[g], count, "sum")
+                sum_grouped = transpose_group(sums[g], count, sum_words, "sum")
                 if g + 1 < len(GROUPS):
                     quantise_later.append(own_codes(GROUPS[g + 1]))
                 sum_q.append(quantise(sum_grouped, count, "sum"))
@@ -219,8 +234,7 @@ def tile_graphsage_pa_t_kernel(tc, nf1, nf2, w1_0, w2_0, out):
             if g > 0:
                 multiply(GROUPS[g - 1], own_q[g - 1], sum_q[g - 1])
             if g + 1 < len(GROUPS):
-                read = sum(GROUPS[g + 1])
-                issue_loads({OWN: read, NEIGHBOUR: read})
+                issue_loads(sum(GROUPS[g + 1]))
             done = sum(GROUPS[g - 1]) if g > 0 else 0
             if done in STORE_ENDS:
                 nc.sync.dma_start(

@@ -8,7 +8,6 @@ BF16 = mybir.dt.bfloat16
 U32 = mybir.dt.uint32
 U8 = mybir.dt.uint8
 FP8X4 = mybir.dt.float8_e4m3fn_x4
-ACT = mybir.ActivationFunctionType
 ALU = mybir.AluOpType
 
 P = 128
@@ -186,10 +185,10 @@ def tile_graphsage_pa_t_kernel(tc, nf1, nf2, w1_0, w2_0, out):
                             start=(i == 0 and g == 0),
                             stop=(i == len(products) - 1 and g == PASSES - 1),
                         )
-            nc.scalar.activation(
+            nc.vector.tensor_scalar_max(
                 out=results[:, first * H : (first + count) * H],
-                in_=acc[:, : count * H],
-                func=ACT.Relu,
+                in0=acc[:, : count * H],
+                scalar1=0.0,
             )
 
         identity = const.tile([P, P], F32, name="identity")
@@ -209,15 +208,16 @@ def tile_graphsage_pa_t_kernel(tc, nf1, nf2, w1_0, w2_0, out):
                 issued[kind].append(first + count)
 
         issue_loads(0)
-        sums = [sum_of_neighbours(GROUPS[0])]
-        w1_q = quantise_weight(nc, const, w1_0, load_in_run_order, copy_of_half, "w1")
-        w2_q = quantise_weight(nc, const, w2_0, load_in_word_order, nc.scalar.copy, "w2")
 
         def own_codes(group):
             grouped = transpose_group(loaded[OWN][group[0]], group[1], own_words, "own")
             return lambda: quantise(grouped, group[1], "own")
 
-        own_q = [own_codes(GROUPS[0])()]
+        quantise_first = own_codes(GROUPS[0])
+        sums = [sum_of_neighbours(GROUPS[0])]
+        w1_q = quantise_weight(nc, const, w1_0, load_in_run_order, copy_of_half, "w1")
+        w2_q = quantise_weight(nc, const, w2_0, load_in_word_order, nc.scalar.copy, "w2")
+        own_q = [quantise_first()]
         sum_q = []
         stored = 0
         for g in range(len(GROUPS) + 1):

@@ -43,7 +43,7 @@ FLOPS = 2 * 2 * NODES * D * H
 
 
 def load_in_word_order(nc, raw, w):
-    nc.scalar.dma_start(
+    nc.sync.dma_start(
         out=raw[:].rearrange("p (g t c) -> p g t c", t=PACK, c=H),
         in_=w.rearrange("(g p t) c -> p g t c", p=P, t=PACK),
     )
@@ -56,12 +56,10 @@ def load_in_run_order(nc, raw, w):
     )
     for g in range(PASSES):
         for u in range(HALVES):
-            nc.scalar.dma_start(out=halves[:, g * HALVES + u, :], in_=rows[g, u])
+            nc.sync.dma_start(out=halves[:, g * HALVES + u, :], in_=rows[g, u])
 
 
-def quantise_weight(nc, const, w, load, copy, name):
-    raw = const.tile([P, PASSES * PACK * H], BF16, name=name + "_raw")
-    load(nc, raw, w)
+def quantise_weight(nc, const, raw, copy, name):
     grouped = const.tile([P, PASSES * H * PACK], BF16, name=name + "_grouped", align_bytes=64)
     copy(
         out=grouped[:].rearrange("p (g c t) -> p g c t", g=PASSES, t=PACK),
@@ -198,15 +196,25 @@ def tile_graphsage_pa_t_kernel(tc, nf1, nf2, w1_0, w2_0, out):
         pending = list(LOADS)
         issued = {OWN: [], NEIGHBOUR: []}
 
+        def load_next():
+            kind, first, count = pending[0]
+            pending.remove(pending[0])
+            load(kind, first, count)
+            issued[kind].append(first + count)
+
         def issue_loads(read):
             while pending:
-                kind, first, count = pending[0]
+                kind = pending[0][0]
                 if len(issued[kind]) >= LOAD_BUFS and issued[kind][-LOAD_BUFS] > read:
                     return
-                pending.remove(pending[0])
-                load(kind, first, count)
-                issued[kind].append(first + count)
+                load_next()
 
+        w1_raw = const.tile([P, PASSES * PACK * H], BF16, name="w1_raw")
+        w2_raw = const.tile([P, PASSES * PACK * H], BF16, name="w2_raw")
+        load_next()
+        load_next()
+        load_in_run_order(nc, w1_raw, w1_0)
+        load_in_word_order(nc, w2_raw, w2_0)
         issue_loads(0)
 
         def own_codes(group):
@@ -215,8 +223,8 @@ def tile_graphsage_pa_t_kernel(tc, nf1, nf2, w1_0, w2_0, out):
 
         quantise_first = own_codes(GROUPS[0])
         sums = [sum_of_neighbours(GROUPS[0])]
-        w1_q = quantise_weight(nc, const, w1_0, load_in_run_order, copy_of_half, "w1")
-        w2_q = quantise_weight(nc, const, w2_0, load_in_word_order, nc.scalar.copy, "w2")
+        w1_q = quantise_weight(nc, const, w1_raw, copy_of_half, "w1")
+        w2_q = quantise_weight(nc, const, w2_raw, nc.scalar.copy, "w2")
         own_q = [quantise_first()]
         sum_q = []
         stored = 0

@@ -31,11 +31,26 @@ GROUPS = [(t, GROUP) for t in range(0, TILES - GROUP, GROUP)] + [
 ]
 
 OWN, NEIGHBOUR = "own", "neighbours"
-LOAD = 2
-LOADS = [
-    (kind, t, LOAD) for t in range(0, TILES - LOAD, LOAD) for kind in (OWN, NEIGHBOUR)
-] + [(OWN, TILES - LOAD, LOAD)] + [(NEIGHBOUR, t, 1) for t in range(TILES - LOAD, TILES)]
-LOAD_BUFS = 8
+SHORT, LONG = 2, 4
+OWN_SIZES = [SHORT] * 2 + [LONG] * 6 + [SHORT] * 2
+NEIGHBOUR_SIZES = [SHORT] * 2 + [LONG] * 3 + [SHORT] * 7 + [1] * 2
+
+
+def load_order():
+    loads = []
+    own_end = neighbour_end = 0
+    own_sizes = list(OWN_SIZES)
+    for count in NEIGHBOUR_SIZES:
+        while own_end < neighbour_end + count:
+            loads.append((OWN, own_end, own_sizes[0]))
+            own_end += own_sizes[0]
+            own_sizes = own_sizes[1:]
+        loads.append((NEIGHBOUR, neighbour_end, count))
+        neighbour_end += count
+    return loads
+
+
+BUFS = {(OWN, SHORT): 4, (OWN, LONG): 3, (NEIGHBOUR, SHORT): 5, (NEIGHBOUR, LONG): 3}
 
 STORE_ENDS = (24, 30, 32)
 
@@ -43,7 +58,7 @@ FLOPS = 2 * 2 * NODES * D * H
 
 
 def load_in_word_order(nc, raw, w):
-    nc.sync.dma_start(
+    nc.scalar.dma_start(
         out=raw[:].rearrange("p (g t c) -> p g t c", t=PACK, c=H),
         in_=w.rearrange("(g p t) c -> p g t c", p=P, t=PACK),
     )
@@ -56,7 +71,7 @@ def load_in_run_order(nc, raw, w):
     )
     for g in range(PASSES):
         for u in range(HALVES):
-            nc.sync.dma_start(out=halves[:, g * HALVES + u, :], in_=rows[g, u])
+            nc.scalar.dma_start(out=halves[:, g * HALVES + u, :], in_=rows[g, u])
 
 
 def quantise_weight(nc, const, raw, copy, name):
@@ -81,20 +96,28 @@ def tile_graphsage_pa_t_kernel(tc, nf1, nf2, w1_0, w2_0, out):
     with ExitStack() as ctx:
         ctx.enter_context(tc.manual_schedule())
         const = ctx.enter_context(tc.tile_pool(name="const", bufs=1))
-        own_pool = ctx.enter_context(tc.tile_pool(name="own_pool", bufs=LOAD_BUFS))
-        neighbour_pool = ctx.enter_context(tc.tile_pool(name="neighbour_pool", bufs=LOAD_BUFS))
+        pools = {
+            (kind, length): ctx.enter_context(
+                tc.tile_pool(name=kind + "_%d" % length, bufs=BUFS[(kind, length)])
+            )
+            for kind, length in BUFS
+        }
         work = ctx.enter_context(tc.tile_pool(name="work", bufs=3))
         psum_t = ctx.enter_context(tc.psum_pool(name="psum_t", bufs=3))
         psum_acc = ctx.enter_context(tc.psum_pool(name="psum_acc", bufs=2))
 
         loaded = {OWN: {}, NEIGHBOUR: {}}
 
+        def length_of(count):
+            return LONG if count > SHORT else SHORT
+
         def load(kind, first, count):
             if kind == OWN:
-                width, rows, pool = D, own_rows, own_pool
+                width, rows = D, own_rows
             else:
-                width, rows, pool = NEIGHBOURS * D, neighbour_rows, neighbour_pool
-            landing = pool.tile([P, LOAD * width], BF16, name=kind)
+                width, rows = NEIGHBOURS * D, neighbour_rows
+            length = length_of(count)
+            landing = pools[(kind, length)].tile([P, length * width], BF16, name=kind)
             nc.sync.dma_start(
                 out=landing[:, : count * width],
                 in_=rows[:, first * width : (first + count) * width],
@@ -193,26 +216,25 @@ def tile_graphsage_pa_t_kernel(tc, nf1, nf2, w1_0, w2_0, out):
         make_identity(nc, identity[:])
         results = const.tile([P, TILES * H], F32, name="results")
 
-        pending = list(LOADS)
-        issued = {OWN: [], NEIGHBOUR: []}
+        pending = load_order()
+        issued = {key: [] for key in BUFS}
 
         def load_next():
             kind, first, count = pending[0]
             pending.remove(pending[0])
             load(kind, first, count)
-            issued[kind].append(first + count)
+            issued[(kind, length_of(count))].append(first + count)
 
         def issue_loads(read):
             while pending:
-                kind = pending[0][0]
-                if len(issued[kind]) >= LOAD_BUFS and issued[kind][-LOAD_BUFS] > read:
+                kind, first, count = pending[0]
+                key = (kind, length_of(count))
+                if len(issued[key]) >= BUFS[key] and issued[key][-BUFS[key]] > read:
                     return
                 load_next()
 
         w1_raw = const.tile([P, PASSES * PACK * H], BF16, name="w1_raw")
         w2_raw = const.tile([P, PASSES * PACK * H], BF16, name="w2_raw")
-        load_next()
-        load_next()
         load_in_run_order(nc, w1_raw, w1_0)
         load_in_word_order(nc, w2_raw, w2_0)
         issue_loads(0)

@@ -8,6 +8,7 @@ BF16 = mybir.dt.bfloat16
 U32 = mybir.dt.uint32
 U8 = mybir.dt.uint8
 FP8X4 = mybir.dt.float8_e4m3fn_x4
+ACT = mybir.ActivationFunctionType
 ALU = mybir.AluOpType
 
 P = 128
@@ -58,7 +59,7 @@ FLOPS = 2 * 2 * NODES * D * H
 
 
 def load_in_word_order(nc, raw, w):
-    nc.scalar.dma_start(
+    nc.sync.dma_start(
         out=raw[:].rearrange("p (g t c) -> p g t c", t=PACK, c=H),
         in_=w.rearrange("(g p t) c -> p g t c", p=P, t=PACK),
     )
@@ -71,15 +72,19 @@ def load_in_run_order(nc, raw, w):
     )
     for g in range(PASSES):
         for u in range(HALVES):
-            nc.scalar.dma_start(out=halves[:, g * HALVES + u, :], in_=rows[g, u])
+            nc.sync.dma_start(out=halves[:, g * HALVES + u, :], in_=rows[g, u])
 
 
-def quantise_weight(nc, const, raw, copy, name):
+def group_features(copy, const, raw, name):
     grouped = const.tile([P, PASSES * H * PACK], BF16, name=name + "_grouped", align_bytes=64)
     copy(
         out=grouped[:].rearrange("p (g c t) -> p g c t", g=PASSES, t=PACK),
         in_=raw[:].rearrange("p (g t c) -> p g c t", g=PASSES, t=PACK),
     )
+    return grouped
+
+
+def quantise_weight(nc, const, grouped, name):
     codes = const.tile([P, PASSES * H], U32, name=name + "_codes", align_bytes=64)
     scales = const.tile([P, PASSES * H], U8, name=name + "_scales", align_bytes=64)
     nc.vector.quantize_mx(out=codes[:].bitcast(FP8X4), scales=scales[:], in_=grouped[:])
@@ -206,11 +211,11 @@ def tile_graphsage_pa_t_kernel(tc, nf1, nf2, w1_0, w2_0, out):
                             start=(i == 0 and g == 0),
                             stop=(i == len(products) - 1 and g == PASSES - 1),
                         )
-            nc.vector.tensor_scalar_max(
-                out=results[:, first * H : (first + count) * H],
-                in0=acc[:, : count * H],
-                scalar1=0.0,
-            )
+            result = results[:, first * H : (first + count) * H]
+            if GROUPS.index(group) % 2 == 0:
+                nc.scalar.activation(out=result, in_=acc[:, : count * H], func=ACT.Relu)
+            else:
+                nc.vector.tensor_scalar_max(out=result, in0=acc[:, : count * H], scalar1=0.0)
 
         identity = const.tile([P, P], F32, name="identity")
         make_identity(nc, identity[:])
@@ -235,39 +240,51 @@ def tile_graphsage_pa_t_kernel(tc, nf1, nf2, w1_0, w2_0, out):
 
         w1_raw = const.tile([P, PASSES * PACK * H], BF16, name="w1_raw")
         w2_raw = const.tile([P, PASSES * PACK * H], BF16, name="w2_raw")
+        load_next()
+        load_next()
         load_in_run_order(nc, w1_raw, w1_0)
         load_in_word_order(nc, w2_raw, w2_0)
         issue_loads(0)
 
-        def own_codes(group):
-            grouped = transpose_group(loaded[OWN][group[0]], group[1], own_words, "own")
-            return lambda: quantise(grouped, group[1], "own")
+        def transpose_own(g):
+            first, count = GROUPS[g]
+            return transpose_group(loaded[OWN][first], count, own_words, "own")
 
-        quantise_first = own_codes(GROUPS[0])
+        def transpose_sums(g):
+            return transpose_group(sums[g], GROUPS[g][1], sum_words, "sum")
+
+        own_grouped = [transpose_own(0)]
         sums = [sum_of_neighbours(GROUPS[0])]
-        w1_q = quantise_weight(nc, const, w1_raw, copy_of_half, "w1")
-        w2_q = quantise_weight(nc, const, w2_raw, nc.scalar.copy, "w2")
-        own_q = [quantise_first()]
-        sum_q = []
+        w1_grouped = group_features(copy_of_half, const, w1_raw, "w1")
+        w1_q = quantise_weight(nc, const, w1_grouped, "w1")
+        own_q = [quantise(own_grouped[0], GROUPS[0][1], "own")]
+        sum_grouped = [transpose_sums(0)]
+        w2_grouped = group_features(nc.scalar.copy, const, w2_raw, "w2")
+        sum_q = [quantise(sum_grouped[0], GROUPS[0][1], "sum")]
+        w2_q = quantise_weight(nc, const, w2_grouped, "w2")
         stored = 0
+        multiplied = 0
         for g in range(len(GROUPS) + 1):
-            quantise_later = []
             if g + 1 < len(GROUPS):
                 sums.append(sum_of_neighbours(GROUPS[g + 1]))
-            if g < len(GROUPS):
-                first, count = GROUPS[g]
-                sum_grouped = transpose_group(sums[g], count, sum_words, "sum")
-                if g + 1 < len(GROUPS):
-                    quantise_later.append(own_codes(GROUPS[g + 1]))
-                sum_q.append(quantise(sum_grouped, count, "sum"))
-                own_q.extend([step() for step in quantise_later])
-            if g > 0:
-                multiply(GROUPS[g - 1], own_q[g - 1], sum_q[g - 1])
+            if 0 < g < len(GROUPS):
+                sum_grouped.append(transpose_sums(g))
+            if g + 1 < len(GROUPS):
+                own_grouped.append(transpose_own(g + 1))
+            if 0 < g < len(GROUPS):
+                sum_q.append(quantise(sum_grouped[g], GROUPS[g][1], "sum"))
+            if g + 1 < len(GROUPS):
+                own_q.append(quantise(own_grouped[g + 1], GROUPS[g + 1][1], "own"))
+            if multiplied < max(g, 1):
+                group = GROUPS[multiplied]
+                multiply(group, own_q[multiplied], sum_q[multiplied])
+                multiplied += 1
+                done = sum(group)
+                if done in STORE_ENDS:
+                    nc.sync.dma_start(
+                        out=out_rows[:, stored * H : done * H],
+                        in_=results[:, stored * H : done * H],
+                    )
+                    stored = done
             if g + 1 < len(GROUPS):
                 issue_loads(sum(GROUPS[g + 1]))
-            done = sum(GROUPS[g - 1]) if g > 0 else 0
-            if done in STORE_ENDS:
-                nc.sync.dma_start(
-                    out=out_rows[:, stored * H : done * H], in_=results[:, stored * H : done * H]
-                )
-                stored = done

from contextlib import ExitStack

import concourse.mybir as mybir
from concourse.masks import make_identity

F32 = mybir.dt.float32
BF16 = mybir.dt.bfloat16
U32 = mybir.dt.uint32
U8 = mybir.dt.uint8
FP8X4 = mybir.dt.float8_e4m3fn_x4
ACT = mybir.ActivationFunctionType
ALU = mybir.AluOpType

P = 128
PACK = 4
K_PASS = P * PACK
HALVES = 2
BLOCK = 32
PAIR = 2

NODES = 4096
NEIGHBOURS = 2
D = 1024
H = 256
PASSES = D // K_PASS
WORDS = D // PAIR

TILES = NODES // P
GROUP = 2
GROUPS = [(t, GROUP) for t in range(0, TILES - GROUP, GROUP)] + [
    (t, 1) for t in range(TILES - GROUP, TILES)
]

OWN, NEIGHBOUR = "own", "neighbours"
SHORT, LONG = 2, 4
OWN_SIZES = [SHORT] * 2 + [LONG] * 6 + [SHORT] * 2
NEIGHBOUR_SIZES = [SHORT] * 2 + [LONG] * 3 + [SHORT] * 7 + [1] * 2


def load_order():
    loads = []
    own_end = neighbour_end = 0
    own_sizes = list(OWN_SIZES)
    for count in NEIGHBOUR_SIZES:
        while own_end < neighbour_end + count:
            loads.append((OWN, own_end, own_sizes[0]))
            own_end += own_sizes[0]
            own_sizes = own_sizes[1:]
        loads.append((NEIGHBOUR, neighbour_end, count))
        neighbour_end += count
    return loads


BUFS = {(OWN, SHORT): 4, (OWN, LONG): 3, (NEIGHBOUR, SHORT): 5, (NEIGHBOUR, LONG): 3}

STORE_ENDS = (24, 30, 32)

FLOPS = 2 * 2 * NODES * D * H


def load_in_word_order(nc, raw, w):
    nc.sync.dma_start(
        out=raw[:].rearrange("p (g t c) -> p g t c", t=PACK, c=H),
        in_=w.rearrange("(g p t) c -> p g t c", p=P, t=PACK),
    )


def load_in_run_order(nc, raw, w):
    halves = raw[:].rearrange("p (s x) -> p s x", s=PASSES * HALVES)
    rows = w.rearrange(
        "(g q u i e) c -> g u q i (e c)", g=PASSES, u=HALVES, i=BLOCK // HALVES // PAIR, e=PAIR
    )
    for g in range(PASSES):
        for u in range(HALVES):
            nc.sync.dma_start(out=halves[:, g * HALVES + u, :], in_=rows[g, u])


def group_features(copy, const, raw, name):
    grouped = const.tile([P, PASSES * H * PACK], BF16, name=name + "_grouped", align_bytes=64)
    copy(
        out=grouped[:].rearrange("p (g c t) -> p g c t", g=PASSES, t=PACK),
        in_=raw[:].rearrange("p (g t c) -> p g c t", g=PASSES, t=PACK),
    )
    return grouped


def quantise_weight(nc, const, grouped, name):
    codes = const.tile([P, PASSES * H], U32, name=name + "_codes", align_bytes=64)
    scales = const.tile([P, PASSES * H], U8, name=name + "_scales", align_bytes=64)
    nc.vector.quantize_mx(out=codes[:].bitcast(FP8X4), scales=scales[:], in_=grouped[:])
    return codes, scales


def tile_graphsage_pa_t_kernel(tc, nf1, nf2, w1_0, w2_0, out):
    nc = tc.nc

    own_rows = nf1.rearrange("(p j) d -> p (j d)", p=P)
    neighbour_rows = nf2.rearrange("(p j) d -> p (j d)", p=P)
    out_rows = out.rearrange("(p j) h -> p (j h)", p=P)

    with ExitStack() as ctx:
        ctx.enter_context(tc.manual_schedule())
        const = ctx.enter_context(tc.tile_pool(name="const", bufs=1))
        pools = {
            (kind, length): ctx.enter_context(
                tc.tile_pool(name=kind + "_%d" % length, bufs=BUFS[(kind, length)])
            )
            for kind, length in BUFS
        }
        work = ctx.enter_context(tc.tile_pool(name="work", bufs=3))
        psum_t = ctx.enter_context(tc.psum_pool(name="psum_t", bufs=3))
        psum_acc = ctx.enter_context(tc.psum_pool(name="psum_acc", bufs=2))

        loaded = {OWN: {}, NEIGHBOUR: {}}

        def length_of(count):
            return LONG if count > SHORT else SHORT

        def load(kind, first, count):
            if kind == OWN:
                width, rows = D, own_rows
            else:
                width, rows = NEIGHBOURS * D, neighbour_rows
            length = length_of(count)
            landing = pools[(kind, length)].tile([P, length * width], BF16, name=kind)
            nc.sync.dma_start(
                out=landing[:, : count * width],
                in_=rows[:, first * width : (first + count) * width],
            )
            for j in range(count):
                loaded[kind][first + j] = (landing, j * width)

        def sum_of_neighbours(group):
            first, count = group
            pair_sum = work.tile([P, GROUP * D], BF16, name="pair_sum")
            for r in range(count):
                landing, column = loaded[NEIGHBOUR][first + r]
                both = landing[:, column : column + NEIGHBOURS * D].rearrange(
                    "p (j b u x) -> p j u b x", j=NEIGHBOURS, u=HALVES, b=D // BLOCK
                )
                nc.vector.tensor_tensor(
                    out=pair_sum[:, r * D : (r + 1) * D].rearrange(
                        "p (u b x) -> p u b x", u=HALVES, b=D // BLOCK
                    ),
                    in0=both[:, 0],
                    in1=both[:, 1],
                    op=ALU.add,
                )
            return pair_sum, 0

        def copy_of_half(out, in_):
            nc.vector.tensor_scalar_mul(out=out, in0=in_, scalar1=1.0 / NEIGHBOURS)

        def own_words(g, u):
            return slice(g * HALVES * P + u, (g + 1) * HALVES * P, HALVES)

        def sum_words(g, u):
            return slice((u * PASSES + g) * P, (u * PASSES + g + 1) * P)

        def transpose_words(rows, column, where, name):
            words = rows[:].bitcast(F32)[:, column // PAIR : column // PAIR + WORDS]
            bank = psum_t.tile([P, WORDS], F32, name=name)
            for g in range(PASSES):
                for u in range(HALVES):
                    nc.tensor.transpose(
                        bank[:, (u * PASSES + g) * P : (u * PASSES + g + 1) * P],
                        words[:, where(g, u)],
                        identity[:],
                    )
            return bank

        def transpose_group(source, count, where, name):
            rows, column = source
            banks = [transpose_words(rows, column + r * D, where, name + "_t") for r in range(count)]
            grouped = work.tile([P, GROUP * D], BF16, name=name + "_grouped", align_bytes=64)
            for r in range(count):
                nc.scalar.copy(
                    out=grouped[:]
                    .bitcast(F32)[:, r * WORDS : (r + 1) * WORDS]
                    .rearrange("p (n u) -> p n u", u=HALVES),
                    in_=banks[r][:].rearrange("p (u n) -> p n u", u=HALVES),
                )
            return grouped

        def quantise(grouped, count, name):
            codes = work.tile([P, GROUP * D // PACK], U32, name=name + "_codes", align_bytes=64)
            scales = work.tile([P, GROUP * D // PACK], U8, name=name + "_scales", align_bytes=64)
            width = count * D // PACK
            nc.vector.quantize_mx(
                out=codes[:, :width].bitcast(FP8X4),
                scales=scales[:, :width],
                in_=grouped[:, : count * D],
            )
            return codes, scales

        def multiply(group, own_q, sum_q):
            first, count = group
            products = ((own_q, w2_q), (sum_q, w1_q))
            acc = psum_acc.tile([P, GROUP * H], F32, name="acc")
            for r in range(count):
                for i, (x_q, w_q) in enumerate(products):
                    for g in range(PASSES):
                        nodes = slice((r * PASSES + g) * P, (r * PASSES + g + 1) * P)
                        cols = slice(g * H, (g + 1) * H)
                        nc.tensor.matmul_mx(
                            out=acc[:, r * H : (r + 1) * H],
                            lhsT=x_q[0][:, nodes].bitcast(FP8X4),
                            lhsT_scale=x_q[1][:, nodes],
                            rhs=w_q[0][:, cols].bitcast(FP8X4),
                            rhs_scale=w_q[1][:, cols],
                            start=(i == 0 and g == 0),
                            stop=(i == len(products) - 1 and g == PASSES - 1),
                        )
            result = results[:, first * H : (first + count) * H]
            if GROUPS.index(group) % 2 == 0:
                nc.scalar.activation(out=result, in_=acc[:, : count * H], func=ACT.Relu)
            else:
                nc.vector.tensor_scalar_max(out=result, in0=acc[:, : count * H], scalar1=0.0)

        identity = const.tile([P, P], F32, name="identity")
        make_identity(nc, identity[:])
        results = const.tile([P, TILES * H], F32, name="results")

        pending = load_order()
        issued = {key: [] for key in BUFS}

        def load_next():
            kind, first, count = pending[0]
            pending.remove(pending[0])
            load(kind, first, count)
            issued[(kind, length_of(count))].append(first + count)

        def issue_loads(read):
            while pending:
                kind, first, count = pending[0]
                key = (kind, length_of(count))
                if len(issued[key]) >= BUFS[key] and issued[key][-BUFS[key]] > read:
                    return
                load_next()

        w1_raw = const.tile([P, PASSES * PACK * H], BF16, name="w1_raw")
        w2_raw = const.tile([P, PASSES * PACK * H], BF16, name="w2_raw")
        load_next()
        load_next()
        load_in_run_order(nc, w1_raw, w1_0)
        load_in_word_order(nc, w2_raw, w2_0)
        issue_loads(0)

        def transpose_own(g):
            first, count = GROUPS[g]
            return transpose_group(loaded[OWN][first], count, own_words, "own")

        def transpose_sums(g):
            return transpose_group(sums[g], GROUPS[g][1], sum_words, "sum")

        own_grouped = [transpose_own(0)]
        sums = [sum_of_neighbours(GROUPS[0])]
        w1_grouped = group_features(copy_of_half, const, w1_raw, "w1")
        w1_q = quantise_weight(nc, const, w1_grouped, "w1")
        own_q = [quantise(own_grouped[0], GROUPS[0][1], "own")]
        sum_grouped = [transpose_sums(0)]
        w2_grouped = group_features(nc.scalar.copy, const, w2_raw, "w2")
        sum_q = [quantise(sum_grouped[0], GROUPS[0][1], "sum")]
        w2_q = quantise_weight(nc, const, w2_grouped, "w2")
        stored = 0
        multiplied = 0
        for g in range(len(GROUPS) + 1):
            if g + 1 < len(GROUPS):
                sums.append(sum_of_neighbours(GROUPS[g + 1]))
            if 0 < g < len(GROUPS):
                sum_grouped.append(transpose_sums(g))
            if g + 1 < len(GROUPS):
                own_grouped.append(transpose_own(g + 1))
            if 0 < g < len(GROUPS):
                sum_q.append(quantise(sum_grouped[g], GROUPS[g][1], "sum"))
            if g + 1 < len(GROUPS):
                own_q.append(quantise(own_grouped[g + 1], GROUPS[g + 1][1], "own"))
            if multiplied < max(g, 1):
                group = GROUPS[multiplied]
                multiply(group, own_q[multiplied], sum_q[multiplied])
                multiplied += 1
                done = sum(group)
                if done in STORE_ENDS:
                    nc.sync.dma_start(
                        out=out_rows[:, stored * H : done * H],
                        in_=results[:, stored * H : done * H],
                    )
                    stored = done
            if g + 1 < len(GROUPS):
                issue_loads(sum(GROUPS[g + 1]))
